import numpy as np
import ml_dtypes


def mxq(x, axis, fmt="e4m3"):
    dtype, down = {"e4m3": (ml_dtypes.float8_e4m3fn, 7), "e5m2": (ml_dtypes.float8_e5m2, 14)}[fmt]
    v = np.moveaxis(np.asarray(x, np.float32).astype(ml_dtypes.bfloat16).astype(np.float64), axis, -1)
    blocks = v.reshape(v.shape[:-1] + (-1, 32))
    amax = np.abs(blocks).max(-1, keepdims=True)
    byte = np.maximum(np.where(amax > 0, np.frexp(amax)[1] - 1 + 127, 0) - down, 1)
    scale = np.exp2(byte - 127.0)
    codes = (blocks / scale).astype(np.float32).astype(dtype).astype(np.float64)
    return np.moveaxis((codes * scale).reshape(v.shape), -1, axis)


WIDE = False


def mx_kscale(k):
    if not WIDE:
        return np.ones(k)
    levels = np.array([10, -10, 5, -5, 0])
    a = np.random.permutation(np.resize(levels, k // 512 * 4)).reshape(k // 512, 4)
    idx = np.arange(k)
    return np.exp2(a[idx // 512, idx % 128 // 32])


BF16 = ml_dtypes.bfloat16


def bf(x):
    return np.asarray(x, np.float32).astype(BF16)


def f64(x):
    return np.asarray(x).astype(np.float64)


M, K, N = 512, 16384, 512
EPS = 1e-05


def setup_inputs():
    s = mx_kscale(K)
    return {"x": bf(np.random.standard_normal((M, K)) * s),
            "weight": bf(np.random.standard_normal((N, K)) / np.sqrt(K) / s[None, :]),
            "bias": bf(np.random.standard_normal(N) * 0.5),
            "gamma": bf(1.0 + 0.1 * np.random.standard_normal(N)),
            "beta": bf(0.1 * np.random.standard_normal(N)),
            "scale": bf(2.0 + 0.1 * np.random.standard_normal(1))}


def reference(x, weight, bias, gamma, beta, scale):
    acc = (mxq(f64(x), 1, "e4m3") @ mxq(f64(weight), 1, "e4m3").T) + f64(bias)[None, :]
    mean = np.mean(acc, axis=1, keepdims=True)
    var = np.mean((acc - mean) ** 2, axis=1, keepdims=True)
    normalized = (acc - mean) / np.sqrt(var + EPS)
    scaled = (normalized * f64(gamma)[None, :] + f64(beta)[None, :]) * f64(scale)[0]
    e = np.exp(scaled - scaled.max(axis=1, keepdims=True))
    return e / e.sum(axis=1, keepdims=True)

@@ -1,0 +1,228 @@
+from contextlib import ExitStack
+
+import concourse.mybir as mybir
+from concourse.masks import make_identity
+
+F32 = mybir.dt.float32
+BF16 = mybir.dt.bfloat16
+U32 = mybir.dt.uint32
+U8 = mybir.dt.uint8
+FP8X4 = mybir.dt.float8_e4m3fn_x4
+ALU = mybir.AluOpType
+ACT = mybir.ActivationFunctionType
+AXIS = mybir.AxisListType
+
+P = 128
+M, N, K = 512, 512, 16384
+EPS = 1e-5
+M_TILES = M // P
+K_PASS = 4 * P
+PASSES = K // K_PASS
+PASS_WORDS = K_PASS // 2
+CHUNK_PASSES = 4
+CHUNK_K = CHUNK_PASSES * K_PASS
+CHUNKS = K // CHUNK_K
+PAIR = 2 * P
+PAIRS = 4
+PAIRS_PER_RUN = 1
+LAST_TILE = M_TILES - 1
+VECTOR_BANK = 1
+
+FLOPS = 2 * M * N * K
+
+
+def tile_modelnew_k_kernel(tc, x, weight, bias, gamma, beta, scale, out):
+    nc = tc.nc
+    with ExitStack() as ctx:
+        const = ctx.enter_context(tc.tile_pool(name="const", bufs=1))
+        keep = ctx.enter_context(tc.tile_pool(name="keep", bufs=1))
+        raw_pool = ctx.enter_context(tc.tile_pool(name="raw", bufs=12))
+        grouped_pool = ctx.enter_context(
+            tc.tile_pool(name="grouped", bufs=2 * PAIRS_PER_RUN * CHUNK_PASSES)
+        )
+        early_pool = ctx.enter_context(tc.tile_pool(name="early", bufs=2))
+        work = ctx.enter_context(tc.tile_pool(name="work", bufs=3))
+        psum_acc = ctx.enter_context(tc.psum_pool(name="psum_acc", bufs=1))
+        psum_bank = ctx.enter_context(tc.psum_pool(name="psum_bank", bufs=4))
+        ctx.enter_context(tc.manual_schedule())
+
+        rows = const.tile([P, 3, N], BF16, name="rows")
+        nc.vector.memset(rows[:], 0.0)
+        for i, vector in enumerate((bias, gamma, beta)):
+            nc.scalar.dma_start(out=rows[0:1, i, :], in_=vector.rearrange("(o n) -> o n", o=1))
+        scale_bf = const.tile([P, 1], BF16, name="scale_bf")
+        nc.scalar.dma_start(out=scale_bf[:], in_=scale.partition_broadcast(P))
+        ident = const.tile([P, P], F32, name="ident")
+        make_identity(nc, ident[:])
+        ones = const.tile([P, P], BF16, name="ones")
+        nc.vector.memset(ones[:], 1.0)
+        neg_half = const.tile([P, M_TILES], F32, name="neg_half")
+        nc.vector.memset(neg_half[:], -0.5)
+
+        warm = const.tile([P, 1], F32, name="warm")
+        nc.vector.memset(warm[:], 0.0)
+        nc.scalar.activation(out=warm[:], in_=warm[:], func=ACT.Exp)
+
+        scale_all = const.tile([P, 1], F32, name="scale_all")
+        nc.vector.tensor_copy(out=scale_all[:], in_=scale_bf[:])
+
+        bias_all = const.tile([P, N], F32, name="bias_all")
+        gain_all = const.tile([P, N], F32, name="gain_all")
+        shift_all = const.tile([P, N], F32, name="shift_all")
+        for i, spread in enumerate((bias_all, gain_all, shift_all)):
+            bank = psum_bank.tile([P, N], F32, name="bank")
+            nc.tensor.matmul(out=bank[:], lhsT=ones[:], rhs=rows[:, i, :], start=True, stop=True)
+            if i == 0:
+                nc.vector.tensor_copy(out=spread[:], in_=bank[:])
+            else:
+                nc.vector.tensor_scalar(
+                    out=spread[:], in0=bank[:], scalar1=scale_all[:, 0:1], scalar2=None, op0=ALU.mult
+                )
+
+        w_codes = keep.tile([P, PASSES, N], U32, name="w_codes", align_bytes=64)
+        w_scales = keep.tile([P, PASSES, N], U8, name="w_scales", align_bytes=64)
+        late_codes = keep.tile([P, PASSES, PAIR], U32, name="late_codes", align_bytes=64)
+        late_scales = keep.tile([P, PASSES, PAIR], U8, name="late_scales", align_bytes=64)
+
+        acc = [psum_acc.tile([P, N], F32, name="acc%d" % mt) for mt in range(M_TILES)]
+
+        def load_and_transpose(source, first_row, c):
+            words = []
+            for a in range(2):
+                raw = raw_pool.tile([P, CHUNK_K], BF16, name="raw")
+                top = first_row + a * P
+                nc.sync.dma_start(
+                    out=raw[:], in_=source[top : top + P, c * CHUNK_K : (c + 1) * CHUNK_K]
+                )
+                words.append(raw[:].bitcast(F32))
+            filled = []
+            for local in range(CHUNK_PASSES):
+                bank = psum_bank.tile([P, 2, 2, P], F32, name="bank")
+                for a in range(2):
+                    for u in range(2):
+                        first = local * PASS_WORDS + u * P
+                        nc.tensor.transpose(bank[:, a, u, :], words[a][:, first : first + P], ident[:])
+                grouped = grouped_pool.tile([P, 4 * PAIR], BF16, name="grouped", align_bytes=64)
+                side_by_side = grouped[:].bitcast(F32).rearrange("p (a r u) -> p a r u", a=2, u=2)
+                halves = bank[:].rearrange("p a u r -> p a r u")
+                if local == VECTOR_BANK:
+                    nc.vector.tensor_copy(out=side_by_side, in_=halves)
+                else:
+                    nc.scalar.copy(out=side_by_side, in_=halves)
+                filled.append(grouped)
+            return filled
+
+        def multiply(g, mt, x_codes, x_scales):
+            cols = slice((mt % 2) * P, (mt % 2) * P + P)
+            nc.tensor.matmul_mx(
+                out=acc[mt][:],
+                lhsT=x_codes[:, cols].bitcast(FP8X4),
+                lhsT_scale=x_scales[:, cols],
+                rhs=w_codes[:, g, :].bitcast(FP8X4),
+                rhs_scale=w_scales[:, g, :],
+                start=(g == 0),
+                stop=(g == PASSES - 1),
+            )
+
+        def multiply_tiles(g, local, early_codes, early_scales, tiles):
+            for mt in tiles:
+                if mt < 2:
+                    multiply(g, mt, early_codes[:, local, :], early_scales[:, local, :])
+                else:
+                    multiply(g, mt, late_codes[:, g, :], late_scales[:, g, :])
+
+        previous = None
+        for c in range(CHUNKS):
+            early_codes = early_pool.tile([P, CHUNK_PASSES, PAIR], U32, name="early_codes", align_bytes=64)
+            early_scales = early_pool.tile([P, CHUNK_PASSES, PAIR], U8, name="early_scales", align_bytes=64)
+            chunk = slice(c * CHUNK_PASSES, (c + 1) * CHUNK_PASSES)
+            pairs = (
+                (weight, 0, w_codes[:, chunk, 0:PAIR], w_scales[:, chunk, 0:PAIR]),
+                (weight, PAIR, w_codes[:, chunk, PAIR:N], w_scales[:, chunk, PAIR:N]),
+                (x, 0, early_codes[:], early_scales[:]),
+                (x, PAIR, late_codes[:, chunk, :], late_scales[:, chunk, :]),
+            )
+            for first_pair in range(0, PAIRS, PAIRS_PER_RUN):
+                run = range(first_pair, first_pair + PAIRS_PER_RUN)
+                filled = [load_and_transpose(pairs[j][0], pairs[j][1], c) for j in run]
+                for j, tiles in zip(run, filled):
+                    for local in range(CHUNK_PASSES):
+                        nc.vector.quantize_mx(
+                            out=pairs[j][2][:, local, :].bitcast(FP8X4),
+                            scales=pairs[j][3][:, local, :],
+                            in_=tiles[local][:],
+                        )
+                if c > 0:
+                    for local in run:
+                        multiply_tiles(
+                            (c - 1) * CHUNK_PASSES + local, local, previous[0], previous[1], range(LAST_TILE)
+                        )
+            previous = (early_codes, early_scales)
+
+        for mt in range(LAST_TILE):
+            for local in range(CHUNK_PASSES):
+                multiply_tiles(
+                    (CHUNKS - 1) * CHUNK_PASSES + local, local, previous[0], previous[1], (mt,)
+                )
+        for g in range(PASSES):
+            multiply(g, LAST_TILE, late_codes[:, g, :], late_scales[:, g, :])
+
+        row_sum = const.tile([P, M_TILES], F32, name="row_sum")
+        neg_mean = const.tile([P, M_TILES], F32, name="neg_mean")
+        square_sum = const.tile([P, M_TILES], F32, name="square_sum")
+        var_eps = const.tile([P, M_TILES], F32, name="var_eps")
+        rstd = const.tile([P, M_TILES], F32, name="rstd")
+        neg_max = const.tile([P, M_TILES], F32, name="neg_max")
+        exp_sum = const.tile([P, M_TILES], F32, name="exp_sum")
+        inv_sum = const.tile([P, M_TILES], F32, name="inv_sum")
+
+        def normalise_and_softmax(tiles):
+            centred = {}
+            for mt in tiles:
+                col = slice(mt, mt + 1)
+                y = work.tile([P, N], F32, name="y")
+                nc.vector.scalar_tensor_tensor(
+                    out=y[:], in0=acc[mt][:], scalar=1.0, in1=bias_all[:],
+                    op0=ALU.mult, op1=ALU.add, accum_out=row_sum[:, col],
+                )
+                nc.vector.tensor_scalar(
+                    out=neg_mean[:, col], in0=row_sum[:, col], scalar1=-1.0 / N, scalar2=None, op0=ALU.mult
+                )
+                squares = work.tile([P, N], F32, name="squares")
+                nc.scalar.activation(
+                    out=squares[:], in_=y[:], func=ACT.Square, bias=neg_mean[:, col],
+                    accum_out=square_sum[:, col],
+                )
+                nc.gpsimd.tensor_scalar(
+                    out=var_eps[:, col], in0=square_sum[:, col], scalar1=1.0 / N, scalar2=EPS,
+                    op0=ALU.mult, op1=ALU.add,
+                )
+                nc.gpsimd.tensor_tensor(
+                    out=rstd[:, col], in0=var_eps[:, col], in1=neg_half[:, col], op=ALU.pow
+                )
+                t = work.tile([P, N], F32, name="t")
+                nc.vector.scalar_tensor_tensor(
+                    out=t[:], in0=y[:], scalar=neg_mean[:, col], in1=gain_all[:], op0=ALU.add, op1=ALU.mult
+                )
+                centred[mt] = t
+            for mt in tiles:
+                col = slice(mt, mt + 1)
+                t = centred[mt]
+                nc.vector.scalar_tensor_tensor(
+                    out=t[:], in0=t[:], scalar=rstd[:, col], in1=shift_all[:], op0=ALU.mult, op1=ALU.add
+                )
+                nc.vector.tensor_reduce(out=neg_max[:, col], in_=t[:], axis=AXIS.X, op=ALU.max, negate=True)
+                nc.scalar.activation(
+                    out=t[:], in_=t[:], func=ACT.Exp, bias=neg_max[:, col], accum_out=exp_sum[:, col]
+                )
+            for mt in tiles:
+                col = slice(mt, mt + 1)
+                t = centred[mt]
+                nc.vector.reciprocal(out=inv_sum[:, col], in_=exp_sum[:, col])
+                nc.vector.tensor_scalar(
+                    out=t[:], in0=t[:], scalar1=inv_sum[:, col], scalar2=None, op0=ALU.mult
+                )
+                nc.sync.dma_start(out=out[mt * P : (mt + 1) * P, :], in_=t[:])
+
+        normalise_and_softmax(range(LAST_TILE))
+        normalise_and_softmax((LAST_TILE,))

@@ -36,7 +36,7 @@ def tile_modelnew_k_kernel(tc, x, weight, bias, gamma, beta, scale, out):
     with ExitStack() as ctx:
         const = ctx.enter_context(tc.tile_pool(name="const", bufs=1))
         keep = ctx.enter_context(tc.tile_pool(name="keep", bufs=1))
-        raw_pool = ctx.enter_context(tc.tile_pool(name="raw", bufs=12))
+        raw_pool = ctx.enter_context(tc.tile_pool(name="raw", bufs=6))
         grouped_pool = ctx.enter_context(
             tc.tile_pool(name="grouped", bufs=2 * PAIRS_PER_RUN * CHUNK_PASSES)
         )
@@ -87,21 +87,21 @@ def tile_modelnew_k_kernel(tc, x, weight, bias, gamma, beta, scale, out):
         acc = [psum_acc.tile([P, N], F32, name="acc%d" % mt) for mt in range(M_TILES)]
 
         def load_and_transpose(source, first_row, c):
-            words = []
-            for a in range(2):
-                raw = raw_pool.tile([P, CHUNK_K], BF16, name="raw")
-                top = first_row + a * P
-                nc.sync.dma_start(
-                    out=raw[:], in_=source[top : top + P, c * CHUNK_K : (c + 1) * CHUNK_K]
-                )
-                words.append(raw[:].bitcast(F32))
+            raw = raw_pool.tile([P, 2, CHUNK_K], BF16, name="raw")
+            nc.sync.dma_start(
+                out=raw[:],
+                in_=source[first_row : first_row + PAIR, c * CHUNK_K : (c + 1) * CHUNK_K].rearrange(
+                    "(a p) k -> p a k", a=2
+                ),
+            )
+            words = raw[:].bitcast(F32)
             filled = []
             for local in range(CHUNK_PASSES):
                 bank = psum_bank.tile([P, 2, 2, P], F32, name="bank")
                 for a in range(2):
                     for u in range(2):
                         first = local * PASS_WORDS + u * P
-                        nc.tensor.transpose(bank[:, a, u, :], words[a][:, first : first + P], ident[:])
+                        nc.tensor.transpose(bank[:, a, u, :], words[:, a, first : first + P], ident[:])
                 grouped = grouped_pool.tile([P, 4 * PAIR], BF16, name="grouped", align_bytes=64)
                 side_by_side = grouped[:].bitcast(F32).rearrange("p (a r u) -> p a r u", a=2, u=2)
                 halves = bank[:].rearrange("p a u r -> p a r u")

from contextlib import ExitStack

import concourse.mybir as mybir
from concourse.masks import make_identity

F32 = mybir.dt.float32
BF16 = mybir.dt.bfloat16
U32 = mybir.dt.uint32
U8 = mybir.dt.uint8
FP8X4 = mybir.dt.float8_e4m3fn_x4
ALU = mybir.AluOpType
ACT = mybir.ActivationFunctionType
AXIS = mybir.AxisListType

P = 128
M, N, K = 512, 512, 16384
EPS = 1e-5
M_TILES = M // P
K_PASS = 4 * P
PASSES = K // K_PASS
PASS_WORDS = K_PASS // 2
CHUNK_PASSES = 4
CHUNK_K = CHUNK_PASSES * K_PASS
CHUNKS = K // CHUNK_K
PAIR = 2 * P
PAIRS = 4
PAIRS_PER_RUN = 1
LAST_TILE = M_TILES - 1
VECTOR_BANK = 1

FLOPS = 2 * M * N * K


def tile_modelnew_k_kernel(tc, x, weight, bias, gamma, beta, scale, out):
    nc = tc.nc
    with ExitStack() as ctx:
        const = ctx.enter_context(tc.tile_pool(name="const", bufs=1))
        keep = ctx.enter_context(tc.tile_pool(name="keep", bufs=1))
        raw_pool = ctx.enter_context(tc.tile_pool(name="raw", bufs=6))
        grouped_pool = ctx.enter_context(
            tc.tile_pool(name="grouped", bufs=2 * PAIRS_PER_RUN * CHUNK_PASSES)
        )
        early_pool = ctx.enter_context(tc.tile_pool(name="early", bufs=2))
        work = ctx.enter_context(tc.tile_pool(name="work", bufs=3))
        psum_acc = ctx.enter_context(tc.psum_pool(name="psum_acc", bufs=1))
        psum_bank = ctx.enter_context(tc.psum_pool(name="psum_bank", bufs=4))
        ctx.enter_context(tc.manual_schedule())

        rows = const.tile([P, 3, N], BF16, name="rows")
        nc.vector.memset(rows[:], 0.0)
        for i, vector in enumerate((bias, gamma, beta)):
            nc.scalar.dma_start(out=rows[0:1, i, :], in_=vector.rearrange("(o n) -> o n", o=1))
        scale_bf = const.tile([P, 1], BF16, name="scale_bf")
        nc.scalar.dma_start(out=scale_bf[:], in_=scale.partition_broadcast(P))
        ident = const.tile([P, P], F32, name="ident")
        make_identity(nc, ident[:])
        ones = const.tile([P, P], BF16, name="ones")
        nc.vector.memset(ones[:], 1.0)
        neg_half = const.tile([P, M_TILES], F32, name="neg_half")
        nc.vector.memset(neg_half[:], -0.5)

        warm = const.tile([P, 1], F32, name="warm")
        nc.vector.memset(warm[:], 0.0)
        nc.scalar.activation(out=warm[:], in_=warm[:], func=ACT.Exp)

        scale_all = const.tile([P, 1], F32, name="scale_all")
        nc.vector.tensor_copy(out=scale_all[:], in_=scale_bf[:])

        bias_all = const.tile([P, N], F32, name="bias_all")
        gain_all = const.tile([P, N], F32, name="gain_all")
        shift_all = const.tile([P, N], F32, name="shift_all")
        for i, spread in enumerate((bias_all, gain_all, shift_all)):
            bank = psum_bank.tile([P, N], F32, name="bank")
            nc.tensor.matmul(out=bank[:], lhsT=ones[:], rhs=rows[:, i, :], start=True, stop=True)
            if i == 0:
                nc.vector.tensor_copy(out=spread[:], in_=bank[:])
            else:
                nc.vector.tensor_scalar(
                    out=spread[:], in0=bank[:], scalar1=scale_all[:, 0:1], scalar2=None, op0=ALU.mult
                )

        w_codes = keep.tile([P, PASSES, N], U32, name="w_codes", align_bytes=64)
        w_scales = keep.tile([P, PASSES, N], U8, name="w_scales", align_bytes=64)
        late_codes = keep.tile([P, PASSES, PAIR], U32, name="late_codes", align_bytes=64)
        late_scales = keep.tile([P, PASSES, PAIR], U8, name="late_scales", align_bytes=64)

        acc = [psum_acc.tile([P, N], F32, name="acc%d" % mt) for mt in range(M_TILES)]

        def load_and_transpose(source, first_row, c):
            raw = raw_pool.tile([P, 2, CHUNK_K], BF16, name="raw")
            nc.sync.dma_start(
                out=raw[:],
                in_=source[first_row : first_row + PAIR, c * CHUNK_K : (c + 1) * CHUNK_K].rearrange(
                    "(a p) k -> p a k", a=2
                ),
            )
            words = raw[:].bitcast(F32)
            filled = []
            for local in range(CHUNK_PASSES):
                bank = psum_bank.tile([P, 2, 2, P], F32, name="bank")
                for a in range(2):
                    for u in range(2):
                        first = local * PASS_WORDS + u * P
                        nc.tensor.transpose(bank[:, a, u, :], words[:, a, first : first + P], ident[:])
                grouped = grouped_pool.tile([P, 4 * PAIR], BF16, name="grouped", align_bytes=64)
                side_by_side = grouped[:].bitcast(F32).rearrange("p (a r u) -> p a r u", a=2, u=2)
                halves = bank[:].rearrange("p a u r -> p a r u")
                if local == VECTOR_BANK:
                    nc.vector.tensor_copy(out=side_by_side, in_=halves)
                else:
                    nc.scalar.copy(out=side_by_side, in_=halves)
                filled.append(grouped)
            return filled

        def multiply(g, mt, x_codes, x_scales):
            cols = slice((mt % 2) * P, (mt % 2) * P + P)
            nc.tensor.matmul_mx(
                out=acc[mt][:],
                lhsT=x_codes[:, cols].bitcast(FP8X4),
                lhsT_scale=x_scales[:, cols],
                rhs=w_codes[:, g, :].bitcast(FP8X4),
                rhs_scale=w_scales[:, g, :],
                start=(g == 0),
                stop=(g == PASSES - 1),
            )

        def multiply_tiles(g, local, early_codes, early_scales, tiles):
            for mt in tiles:
                if mt < 2:
                    multiply(g, mt, early_codes[:, local, :], early_scales[:, local, :])
                else:
                    multiply(g, mt, late_codes[:, g, :], late_scales[:, g, :])

        previous = None
        for c in range(CHUNKS):
            early_codes = early_pool.tile([P, CHUNK_PASSES, PAIR], U32, name="early_codes", align_bytes=64)
            early_scales = early_pool.tile([P, CHUNK_PASSES, PAIR], U8, name="early_scales", align_bytes=64)
            chunk = slice(c * CHUNK_PASSES, (c + 1) * CHUNK_PASSES)
            pairs = (
                (weight, 0, w_codes[:, chunk, 0:PAIR], w_scales[:, chunk, 0:PAIR]),
                (weight, PAIR, w_codes[:, chunk, PAIR:N], w_scales[:, chunk, PAIR:N]),
                (x, 0, early_codes[:], early_scales[:]),
                (x, PAIR, late_codes[:, chunk, :], late_scales[:, chunk, :]),
            )
            for first_pair in range(0, PAIRS, PAIRS_PER_RUN):
                run = range(first_pair, first_pair + PAIRS_PER_RUN)
                filled = [load_and_transpose(pairs[j][0], pairs[j][1], c) for j in run]
                for j, tiles in zip(run, filled):
                    for local in range(CHUNK_PASSES):
                        nc.vector.quantize_mx(
                            out=pairs[j][2][:, local, :].bitcast(FP8X4),
                            scales=pairs[j][3][:, local, :],
                            in_=tiles[local][:],
                        )
                if c > 0:
                    for local in run:
                        multiply_tiles(
                            (c - 1) * CHUNK_PASSES + local, local, previous[0], previous[1], range(LAST_TILE)
                        )
            previous = (early_codes, early_scales)

        for mt in range(LAST_TILE):
            for local in range(CHUNK_PASSES):
                multiply_tiles(
                    (CHUNKS - 1) * CHUNK_PASSES + local, local, previous[0], previous[1], (mt,)
                )
        for g in range(PASSES):
            multiply(g, LAST_TILE, late_codes[:, g, :], late_scales[:, g, :])

        row_sum = const.tile([P, M_TILES], F32, name="row_sum")
        neg_mean = const.tile([P, M_TILES], F32, name="neg_mean")
        square_sum = const.tile([P, M_TILES], F32, name="square_sum")
        var_eps = const.tile([P, M_TILES], F32, name="var_eps")
        rstd = const.tile([P, M_TILES], F32, name="rstd")
        neg_max = const.tile([P, M_TILES], F32, name="neg_max")
        exp_sum = const.tile([P, M_TILES], F32, name="exp_sum")
        inv_sum = const.tile([P, M_TILES], F32, name="inv_sum")

        def normalise_and_softmax(tiles):
            centred = {}
            for mt in tiles:
                col = slice(mt, mt + 1)
                y = work.tile([P, N], F32, name="y")
                nc.vector.scalar_tensor_tensor(
                    out=y[:], in0=acc[mt][:], scalar=1.0, in1=bias_all[:],
                    op0=ALU.mult, op1=ALU.add, accum_out=row_sum[:, col],
                )
                nc.vector.tensor_scalar(
                    out=neg_mean[:, col], in0=row_sum[:, col], scalar1=-1.0 / N, scalar2=None, op0=ALU.mult
                )
                squares = work.tile([P, N], F32, name="squares")
                nc.scalar.activation(
                    out=squares[:], in_=y[:], func=ACT.Square, bias=neg_mean[:, col],
                    accum_out=square_sum[:, col],
                )
                nc.gpsimd.tensor_scalar(
                    out=var_eps[:, col], in0=square_sum[:, col], scalar1=1.0 / N, scalar2=EPS,
                    op0=ALU.mult, op1=ALU.add,
                )
                nc.gpsimd.tensor_tensor(
                    out=rstd[:, col], in0=var_eps[:, col], in1=neg_half[:, col], op=ALU.pow
                )
                t = work.tile([P, N], F32, name="t")
                nc.vector.scalar_tensor_tensor(
                    out=t[:], in0=y[:], scalar=neg_mean[:, col], in1=gain_all[:], op0=ALU.add, op1=ALU.mult
                )
                centred[mt] = t
            for mt in tiles:
                col = slice(mt, mt + 1)
                t = centred[mt]
                nc.vector.scalar_tensor_tensor(
                    out=t[:], in0=t[:], scalar=rstd[:, col], in1=shift_all[:], op0=ALU.mult, op1=ALU.add
                )
                nc.vector.tensor_reduce(out=neg_max[:, col], in_=t[:], axis=AXIS.X, op=ALU.max, negate=True)
                nc.scalar.activation(
                    out=t[:], in_=t[:], func=ACT.Exp, bias=neg_max[:, col], accum_out=exp_sum[:, col]
                )
            for mt in tiles:
                col = slice(mt, mt + 1)
                t = centred[mt]
                nc.vector.reciprocal(out=inv_sum[:, col], in_=exp_sum[:, col])
                nc.vector.tensor_scalar(
                    out=t[:], in0=t[:], scalar1=inv_sum[:, col], scalar2=None, op0=ALU.mult
                )
                nc.sync.dma_start(out=out[mt * P : (mt + 1) * P, :], in_=t[:])

        normalise_and_softmax(range(LAST_TILE))
        normalise_and_softmax((LAST_TILE,))
